import numpy as np
import ml_dtypes

BF16 = ml_dtypes.bfloat16


def bf(x):
    return np.asarray(x, np.float32).astype(BF16)


def f32(x):
    return np.asarray(x, np.float32)


def f64(x):
    return np.asarray(x).astype(np.float64)


def striped(idx):
    return np.tile(idx.reshape(-1, 16).T, (8, 1))


C, S, N = 1024, 256, 1024


def setup_inputs():
    return {"weight": f32(np.random.uniform(-1.0, 1.0, (C, S))), "offs": striped(np.concatenate([np.random.permutation(S) for _ in range(-(-(N) // S))])[:N])}


def reference(weight, offs):
    idx = offs[:16].T.reshape(-1)
    return f64(weight)[:, idx]

@@ -1,0 +1,39 @@
+import concourse.mybir as mybir
+
+F32 = mybir.dt.float32
+U16 = mybir.dt.uint16
+COPY = mybir.ActivationFunctionType.Copy
+
+P = 128
+PER_COLUMN = 16
+
+
+def tile_embedding2d_kernel(tc, weight, offs, out):
+    nc = tc.nc
+    channels, codes = weight.shape
+    places = out.shape[1]
+    blocks = channels // P
+    piece = codes
+    pieces = places // piece
+    piece_columns = piece // PER_COLUMN
+
+    with (
+        tc.tile_pool(name="held", bufs=1) as held,
+        tc.tile_pool(name="results", bufs=blocks) as results,
+    ):
+        offsets = held.tile([P, places // PER_COLUMN], U16, name="offsets")
+        nc.sync.dma_start(offsets[:], offs)
+
+        for b in range(blocks):
+            rows = slice(b * P, (b + 1) * P)
+            table = held.tile([P, codes], F32, name=f"table{b}")
+            nc.sync.dma_start(table[:], weight[rows, :])
+
+            picked = results.tile([P, places], F32, name="picked")
+            for k in range(pieces):
+                nc.scalar.activation(
+                    picked[:, k * piece : (k + 1) * piece],
+                    table[:].indirect(offsets[:, k * piece_columns : (k + 1) * piece_columns]),
+                    COPY,
+                )
+            nc.sync.dma_start(out[rows, :], picked[:])

@@ -19,7 +19,7 @@ def tile_embedding2d_kernel(tc, weight, offs, out):
 
     with (
         tc.tile_pool(name="held", bufs=1) as held,
-        tc.tile_pool(name="results", bufs=blocks) as results,
+        tc.tile_pool(name="results", bufs=blocks * pieces) as results,
     ):
         offsets = held.tile([P, places // PER_COLUMN], U16, name="offsets")
         nc.sync.dma_start(offsets[:], offs)
@@ -29,11 +29,11 @@ def tile_embedding2d_kernel(tc, weight, offs, out):
             table = held.tile([P, codes], F32, name=f"table{b}")
             nc.sync.dma_start(table[:], weight[rows, :])
 
-            picked = results.tile([P, places], F32, name="picked")
             for k in range(pieces):
+                picked = results.tile([P, piece], F32, name="picked")
                 nc.scalar.activation(
-                    picked[:, k * piece : (k + 1) * piece],
+                    picked[:],
                     table[:].indirect(offsets[:, k * piece_columns : (k + 1) * piece_columns]),
                     COPY,
                 )
-            nc.sync.dma_start(out[rows, :], picked[:])
+                nc.sync.dma_start(out[rows, k * piece : (k + 1) * piece], picked[:])

@@ -19,21 +19,25 @@ def tile_embedding2d_kernel(tc, weight, offs, out):
 
     with (
         tc.tile_pool(name="held", bufs=1) as held,
-        tc.tile_pool(name="results", bufs=blocks * pieces) as results,
+        tc.tile_pool(name="results", bufs=blocks) as results,
     ):
         offsets = held.tile([P, places // PER_COLUMN], U16, name="offsets")
         nc.sync.dma_start(offsets[:], offs)
+
+        warm = held.tile([P, 8], F32, name="warm")
+        nc.vector.memset(warm[:], 0.0)
+        nc.scalar.activation(warm[:], warm[:], COPY)
 
         for b in range(blocks):
             rows = slice(b * P, (b + 1) * P)
             table = held.tile([P, codes], F32, name=f"table{b}")
             nc.sync.dma_start(table[:], weight[rows, :])
 
+            picked = results.tile([P, places], F32, name="picked")
             for k in range(pieces):
-                picked = results.tile([P, piece], F32, name="picked")
                 nc.scalar.activation(
-                    picked[:],
+                    picked[:, k * piece : (k + 1) * piece],
                     table[:].indirect(offsets[:, k * piece_columns : (k + 1) * piece_columns]),
                     COPY,
                 )
-                nc.sync.dma_start(out[rows, k * piece : (k + 1) * piece], picked[:])
+            nc.sync.dma_start(out[rows, :], picked[:])

@@ -24,20 +24,22 @@ def tile_embedding2d_kernel(tc, weight, offs, out):
         offsets = held.tile([P, places // PER_COLUMN], U16, name="offsets")
         nc.sync.dma_start(offsets[:], offs)
 
+        tables = []
+        for b in range(blocks):
+            table = held.tile([P, codes], F32, name=f"table{b}")
+            nc.sync.dma_start(table[:], weight[b * P : (b + 1) * P, :])
+            tables.append(table)
+
         warm = held.tile([P, 8], F32, name="warm")
         nc.vector.memset(warm[:], 0.0)
         nc.scalar.activation(warm[:], warm[:], COPY)
 
         for b in range(blocks):
-            rows = slice(b * P, (b + 1) * P)
-            table = held.tile([P, codes], F32, name=f"table{b}")
-            nc.sync.dma_start(table[:], weight[rows, :])
-
             picked = results.tile([P, places], F32, name="picked")
             for k in range(pieces):
                 nc.scalar.activation(
                     picked[:, k * piece : (k + 1) * piece],
-                    table[:].indirect(offsets[:, k * piece_columns : (k + 1) * piece_columns]),
+                    tables[b][:].indirect(offsets[:, k * piece_columns : (k + 1) * piece_columns]),
                     COPY,
                 )
-            nc.sync.dma_start(out[rows, :], picked[:])
+            nc.sync.dma_start(out[b * P : (b + 1) * P, :], picked[:])

@@ -35,11 +35,17 @@ def tile_embedding2d_kernel(tc, weight, offs, out):
         nc.scalar.activation(warm[:], warm[:], COPY)
 
         for b in range(blocks):
+            rows = slice(b * P, (b + 1) * P)
+            last_block = b == blocks - 1
             picked = results.tile([P, places], F32, name="picked")
             for k in range(pieces):
+                columns = slice(k * piece, (k + 1) * piece)
                 nc.scalar.activation(
-                    picked[:, k * piece : (k + 1) * piece],
+                    picked[:, columns],
                     tables[b][:].indirect(offsets[:, k * piece_columns : (k + 1) * piece_columns]),
                     COPY,
                 )
-            nc.sync.dma_start(out[b * P : (b + 1) * P, :], picked[:])
+                if last_block:
+                    nc.sync.dma_start(out[rows, columns], picked[:, columns])
+            if not last_block:
+                nc.sync.dma_start(out[rows, :], picked[:])

@@ -22,13 +22,14 @@ def tile_embedding2d_kernel(tc, weight, offs, out):
         tc.tile_pool(name="results", bufs=blocks) as results,
     ):
         offsets = held.tile([P, places // PER_COLUMN], U16, name="offsets")
-        nc.sync.dma_start(offsets[:], offs)
 
         tables = []
         for b in range(blocks):
             table = held.tile([P, codes], F32, name=f"table{b}")
             nc.sync.dma_start(table[:], weight[b * P : (b + 1) * P, :])
             tables.append(table)
+            if b == 0:
+                nc.sync.dma_start(offsets[:], offs)
 
         warm = held.tile([P, 8], F32, name="warm")
         nc.vector.memset(warm[:], 0.0)

import concourse.mybir as mybir

F32 = mybir.dt.float32
U16 = mybir.dt.uint16
COPY = mybir.ActivationFunctionType.Copy

P = 128
PER_COLUMN = 16


def tile_embedding2d_kernel(tc, weight, offs, out):
    nc = tc.nc
    channels, codes = weight.shape
    places = out.shape[1]
    blocks = channels // P
    piece = codes
    pieces = places // piece
    piece_columns = piece // PER_COLUMN

    with (
        tc.tile_pool(name="held", bufs=1) as held,
        tc.tile_pool(name="results", bufs=blocks) as results,
    ):
        offsets = held.tile([P, places // PER_COLUMN], U16, name="offsets")

        tables = []
        for b in range(blocks):
            table = held.tile([P, codes], F32, name=f"table{b}")
            nc.sync.dma_start(table[:], weight[b * P : (b + 1) * P, :])
            tables.append(table)
            if b == 0:
                nc.sync.dma_start(offsets[:], offs)

        warm = held.tile([P, 8], F32, name="warm")
        nc.vector.memset(warm[:], 0.0)
        nc.scalar.activation(warm[:], warm[:], COPY)

        for b in range(blocks):
            rows = slice(b * P, (b + 1) * P)
            last_block = b == blocks - 1
            picked = results.tile([P, places], F32, name="picked")
            for k in range(pieces):
                columns = slice(k * piece, (k + 1) * piece)
                nc.scalar.activation(
                    picked[:, columns],
                    tables[b][:].indirect(offsets[:, k * piece_columns : (k + 1) * piece_columns]),
                    COPY,
                )
                if last_block:
                    nc.sync.dma_start(out[rows, columns], picked[:, columns])
            if not last_block:
                nc.sync.dma_start(out[rows, :], picked[:])
